import numpy as np
import ml_dtypes


def mxq(x, axis, fmt="e4m3"):
    dtype, down = {"e4m3": (ml_dtypes.float8_e4m3fn, 7), "e5m2": (ml_dtypes.float8_e5m2, 14)}[fmt]
    v = np.moveaxis(np.asarray(x, np.float32).astype(ml_dtypes.bfloat16).astype(np.float64), axis, -1)
    blocks = v.reshape(v.shape[:-1] + (-1, 32))
    amax = np.abs(blocks).max(-1, keepdims=True)
    byte = np.maximum(np.where(amax > 0, np.frexp(amax)[1] - 1 + 127, 0) - down, 1)
    scale = np.exp2(byte - 127.0)
    codes = (blocks / scale).astype(np.float32).astype(dtype).astype(np.float64)
    return np.moveaxis((codes * scale).reshape(v.shape), -1, axis)


WIDE = False


def mx_kscale(k):
    if not WIDE:
        return np.ones(k)
    levels = np.array([10, -10, 5, -5, 0])
    a = np.random.permutation(np.resize(levels, k // 512 * 4)).reshape(k // 512, 4)
    idx = np.arange(k)
    return np.exp2(a[idx // 512, idx % 128 // 32])


BF16 = ml_dtypes.bfloat16


def bf(x):
    return np.asarray(x, np.float32).astype(BF16)


def f64(x):
    return np.asarray(x).astype(np.float64)


E2M1 = np.array([0.0, 0.5, 1.0, 1.5, 2.0, 3.0, 4.0, 6.0, -0.0, -0.5, -1.0, -1.5, -2.0, -3.0, -4.0, -6.0])


def pack_weight(w, fmt):
    k, n = w.shape
    w = f64(bf(w)).reshape(k // 32, 32, n)
    amax = np.abs(w).max(1)
    if fmt == "e4m3":
        byte = np.frexp(amax)[1] - 1 + 127 - 7
    else:
        mant, ex = np.frexp(amax / 6.0)
        byte = np.where(mant > 0.5, ex, ex - 1) + 127
    byte = np.clip(np.where(amax > 0, byte, 1), 1, 254)
    scaled = (w * np.exp2(127.0 - byte)[:, None, :]).reshape(k, n).astype(np.float32)
    by_word = np.ascontiguousarray(scaled.reshape(k // 512, 128, 4, n).transpose(0, 1, 3, 2))
    if fmt == "e4m3":
        words = by_word.astype(ml_dtypes.float8_e4m3fn).view(np.uint8)
    else:
        c = by_word.astype(ml_dtypes.float4_e2m1fn).view(np.uint8) & 0xF
        words = c[..., 0::2] | (c[..., 1::2] << 4)
    return np.ascontiguousarray(words), np.ascontiguousarray(byte.astype(np.uint8).reshape(k // 512, 16, n))


def unpack_weight(words, scales, fmt):
    g, p, n, _ = words.shape
    if fmt == "e4m3":
        vals = np.ascontiguousarray(words).view(ml_dtypes.float8_e4m3fn).astype(np.float64)
    else:
        nib = np.empty((g, p, n, 4), np.uint8)
        nib[..., 0::2] = words & 0xF
        nib[..., 1::2] = words >> 4
        vals = E2M1[nib]
    vals = vals * np.repeat(np.exp2(scales.astype(np.float64) - 127.0), 8, axis=1)[..., None]
    return vals.transpose(0, 1, 3, 2).reshape(g * 512, n)

def pack4(w):
    words, scales = pack_weight(w, "e2m1")
    return words.reshape(words.shape[0], 128, -1), scales


def unpack4(words, scales):
    return unpack_weight(words.reshape(words.shape[0], 128, -1, 2), scales, "e2m1")


B, T, C, HS, DW, DA, DV, DG = 2, 256, 512, 64, 128, 128, 128, 256


def sigmoid(z):
    return 1.0 / (1.0 + np.exp(-z))


def setup_inputs():
    s = mx_kscale(C)
    x = bf(np.random.standard_normal((B, T, C)) * s)
    v_first = bf(np.random.standard_normal((B, T, C)))
    x_v = bf(np.random.uniform(0.0, 1.0, C))
    Wv = np.random.standard_normal((C, C)) / np.sqrt(C) / s[None, :]
    Wv_words, Wv_scales = pack4(np.ascontiguousarray(Wv.T))
    v0 = bf(np.random.standard_normal(C))
    xv_v1 = bf(0.8 * np.random.standard_normal((B, T, DV)))
    v2 = bf(np.random.standard_normal((DV, C)) / np.sqrt(DV))
    return {
        "x": x,
        "v_first": v_first,
        "x_v": x_v,
        "Wv_words": Wv_words,
        "Wv_scales": Wv_scales,
        "v0": v0,
        "xv_v1": xv_v1,
        "v2": v2,
    }


def reference(x, v_first, x_v, Wv_words, Wv_scales, v0, xv_v1, v2):
    x = f64(x)
    xprev = np.concatenate([np.zeros_like(x[:, :1]), x[:, :-1]], axis=1)
    xx = xprev - x
    xv = x + xx * f64(x_v)
    v = mxq(xv, 2, "e4m3") @ unpack4(Wv_words, Wv_scales)
    v = v + (f64(v_first) - v) * sigmoid(f64(v0) + f64(xv_v1) @ f64(v2))
    return v

@@ -1,0 +1,226 @@
+import concourse.mybir as mybir
+from concourse.masks import make_identity
+
+F32 = mybir.dt.float32
+BF16 = mybir.dt.bfloat16
+I32 = mybir.dt.int32
+U32 = mybir.dt.uint32
+U8 = mybir.dt.uint8
+FP8X4 = mybir.dt.float8_e4m3fn_x4
+FP4X4 = mybir.dt.float4_e2m1fn_x4
+ALU = mybir.AluOpType
+ACT = mybir.ActivationFunctionType
+
+P = 128
+PACK = 4
+SEQS = 2
+T = 256
+C = 512
+DV = 128
+HALVES = T // P
+TILES = SEQS * HALVES
+N_TILES = C // P
+WORDS = C // 2
+
+FLOPS = 2 * SEQS * T * C * C + 2 * SEQS * T * DV * C
+
+
+def tile_full_tmix_params_pb_s_kernel(
+    tc, x, v_first, x_v, Wv_words, Wv_scales, v0, xv_v1, v2, out
+):
+    nc = tc.nc
+    x_view = x.flatten_outer_dims().rearrange("(i p) c -> p i c", p=P)
+    vf_view = v_first.flatten_outer_dims().rearrange("(i p) c -> p i c", p=P)
+    v1_view = xv_v1.flatten_outer_dims().rearrange("(i p) d -> p i d", p=P)
+    out_view = out.flatten_outer_dims().rearrange("(i p) n -> p i n", p=P)
+
+    with tc.tile_pool(name="keep", bufs=1) as keep, tc.psum_pool(
+        name="banks", bufs=1
+    ) as banks, tc.manual_schedule():
+        mix_bf = keep.tile([P, PACK], BF16)
+        nc.scalar.dma_start(out=mix_bf[:], in_=x_v.rearrange("(p t) -> p t", t=PACK))
+        bias = keep.tile([P, N_TILES], BF16)
+        with nc.allow_non_contiguous_dma(reason="512 values, one to a partition and column"):
+            nc.scalar.dma_start(out=bias[:], in_=v0.rearrange("(j p) -> p j", p=P))
+
+        x_sb = keep.tile([P, TILES, C], BF16)
+        for b in range(SEQS):
+            tiles_of_b = slice(b * HALVES, (b + 1) * HALVES)
+            nc.sync.dma_start(out=x_sb[:, tiles_of_b, :], in_=x_view[:, tiles_of_b, :])
+        v1_sb = keep.tile([P, TILES, DV], BF16)
+        nc.sync.dma_start(out=v1_sb[:], in_=v1_view)
+        v2_sb = keep.tile([P, C], BF16)
+        nc.sync.dma_start(out=v2_sb[:], in_=v2)
+        w_words = keep.tile([P, 2 * C], U8, align_bytes=64)
+        nc.sync.dma_start(out=w_words[:].bitcast(I32), in_=Wv_words[0].bitcast(I32))
+        w_scales = keep.tile([P, C], U8, align_bytes=64)
+        nc.vector.memset(w_scales[:].bitcast(I32), 0)
+        for quadrant in range(4):
+            nc.sync.dma_start(
+                out=w_scales[32 * quadrant : 32 * quadrant + 4, :].bitcast(I32),
+                in_=Wv_scales[0, 4 * quadrant : 4 * quadrant + 4, :].bitcast(I32),
+            )
+        vf_sb = keep.tile([P, TILES, C], BF16)
+        nc.sync.dma_start(out=vf_sb[:], in_=vf_view)
+
+        ident_f32 = keep.tile([P, P], F32)
+        make_identity(nc, ident_f32[:])
+        ident_bf = keep.tile([P, P], BF16)
+        make_identity(nc, ident_bf[:])
+        prev_part = keep.tile([P, SEQS, PACK, T], F32)
+        nc.gpsimd.memset(prev_part[:, :, :, 0:8], 0.0)
+        warm_in = keep.tile([P, 1], F32)
+        nc.vector.memset(warm_in[:], 0.0)
+        warm_out = keep.tile([P, 1], F32)
+        nc.scalar.activation(out=warm_out[:], in_=warm_in[:], func=ACT.Sigmoid)
+        mix_prev = keep.tile([P, PACK], F32)
+        nc.vector.tensor_copy(out=mix_prev[:], in_=mix_bf[:])
+        mix_cur = keep.tile([P, PACK], F32)
+        nc.vector.tensor_scalar(
+            out=mix_cur[:], in0=mix_bf[:], scalar1=-1.0, scalar2=1.0, op0=ALU.mult, op1=ALU.add
+        )
+
+        xt_scalar = []
+        xt_vector = []
+        for b in range(SEQS):
+            xt_s = banks.tile([P, 2, T], F32, name="xt_s%d" % b, tag="bank%d" % (2 * b))
+            xt_v = banks.tile([P, 2, T], F32, name="xt_v%d" % b, tag="bank%d" % (2 * b + 1))
+            xt_scalar.append(xt_s)
+            xt_vector.append(xt_v)
+
+        x_words = x_sb[:].bitcast(F32)
+        for b in range(SEQS):
+            for bank in (xt_scalar[b], xt_vector[b]):
+                for u in range(2):
+                    for h in range(HALVES):
+                        nc.tensor.transpose(
+                            bank[:, u, h * P : (h + 1) * P],
+                            x_words[:, b * HALVES + h, u:WORDS:2],
+                            ident_f32[:],
+                        )
+
+        def channel_plane(bank, t):
+            halves = bank[:].bitcast(BF16).rearrange("p u (c e) -> p u c e", e=2)
+            return halves[:, t // 2, :, t % 2]
+
+        planes = []
+        grouped = []
+        codes = []
+        code_scales = []
+        for b in range(SEQS):
+            planes.append(keep.tile([P, PACK, T], BF16, name="planes%d" % b))
+            grouped.append(keep.tile([P, T, PACK], BF16, name="grouped%d" % b, align_bytes=64))
+            codes.append(keep.tile([P, T], U32, name="codes%d" % b, align_bytes=64))
+            code_scales.append(keep.tile([P, T], U8, name="code_scales%d" % b, align_bytes=64))
+
+        def mix(b):
+            for t in range(PACK):
+                nc.scalar.activation(
+                    out=prev_part[:, b, t, 1:T],
+                    in_=channel_plane(xt_scalar[b], t)[:, 0 : T - 1],
+                    func=ACT.Copy,
+                    scale=mix_prev[:, t : t + 1],
+                )
+                nc.vector.scalar_tensor_tensor(
+                    out=planes[b][:, t, :],
+                    in0=channel_plane(xt_vector[b], t),
+                    scalar=mix_cur[:, t : t + 1],
+                    in1=prev_part[:, b, t, :],
+                    op0=ALU.mult,
+                    op1=ALU.add,
+                )
+
+        def group(b):
+            nc.vector.tensor_copy(out=grouped[b][:], in_=planes[b][:].rearrange("p t c -> p c t"))
+
+        def quantise(b):
+            nc.vector.quantize_mx(
+                out=codes[b][:].bitcast(FP8X4),
+                scales=code_scales[b][:],
+                in_=grouped[b][:].rearrange("p c t -> p (c t)"),
+            )
+
+        product = [None] * TILES
+
+        def multiply(b):
+            for h in range(HALVES):
+                i = b * HALVES + h
+                product[i] = banks.tile([P, C], F32, name="product%d" % i, tag="bank%d" % i)
+                tokens = slice(h * P, (h + 1) * P)
+                nc.tensor.matmul_mx(
+                    out=product[i][:],
+                    lhsT=codes[b][:, tokens].bitcast(FP8X4),
+                    lhsT_scale=code_scales[b][:, tokens],
+                    rhs=w_words[:].bitcast(FP4X4),
+                    rhs_scale=w_scales[:],
+                    start=True,
+                    stop=True,
+                )
+
+        diff = []
+        step = []
+        result = []
+        for i in range(TILES):
+            diff.append(keep.tile([P, C], F32, name="diff%d" % i))
+            step.append(keep.tile([P, C], F32, name="step%d" % i))
+            result.append(keep.tile([P, C], F32, name="result%d" % i))
+
+        def subtract(i):
+            nc.vector.tensor_tensor(
+                out=diff[i][:], in0=vf_sb[:, i, :], in1=product[i][:], op=ALU.subtract
+            )
+
+        mix(0)
+        v1t_ps = banks.tile([P, TILES * P], BF16, name="v1t_ps", tag="bank4")
+        for i in range(TILES):
+            nc.tensor.transpose(v1t_ps[:, i * P : (i + 1) * P], v1_sb[:, i, :], ident_bf[:])
+        group(0)
+        v1t = keep.tile([P, TILES * P], BF16)
+        nc.vector.tensor_copy(out=v1t[:], in_=v1t_ps[:])
+        quantise(0)
+
+        logit = []
+        for j in range(N_TILES):
+            logit_j = banks.tile([P, TILES * P], F32, name="logit%d" % j, tag="bank%d" % (4 + j))
+            nc.tensor.matmul(
+                out=logit_j[:], lhsT=v2_sb[:, j * P : (j + 1) * P], rhs=v1t[:], start=True, stop=True
+            )
+            logit.append(logit_j)
+
+        mix(1)
+        multiply(0)
+
+        gate_t = keep.tile([P, N_TILES, TILES * P], F32)
+        for j in range(N_TILES):
+            nc.scalar.activation(
+                out=gate_t[:, j, :], in_=logit[j][:], func=ACT.Sigmoid, bias=bias[:, j : j + 1]
+            )
+
+        group(1)
+        subtract(0)
+        quantise(1)
+        subtract(1)
+        multiply(1)
+        subtract(2)
+        subtract(3)
+
+        gate = []
+        for i in range(TILES):
+            gate_i = banks.tile([P, C], F32, name="gate%d" % i, tag="bank%d" % (4 + i))
+            for j in range(N_TILES):
+                nc.tensor.transpose(
+                    gate_i[:, j * P : (j + 1) * P], gate_t[:, j, i * P : (i + 1) * P], ident_f32[:]
+                )
+            gate.append(gate_i)
+
+        def finish(i):
+            nc.vector.tensor_tensor(
+                out=result[i][:], in0=step[i][:], in1=product[i][:], op=ALU.add
+            )
+            nc.sync.dma_start(out=out_view[:, i, :], in_=result[i][:])
+
+        for i in range(TILES):
+            nc.vector.tensor_tensor(out=step[i][:], in0=diff[i][:], in1=gate[i][:], op=ALU.mult)
+            if i > 0:
+                finish(i - 1)
+        finish(TILES - 1)

@@ -80,28 +80,26 @@ def tile_full_tmix_params_pb_s_kernel(
             out=mix_cur[:], in0=mix_bf[:], scalar1=-1.0, scalar2=1.0, op0=ALU.mult, op1=ALU.add
         )
 
-        xt_scalar = []
-        xt_vector = []
+        xt = []
         for b in range(SEQS):
-            xt_s = banks.tile([P, 2, T], F32, name="xt_s%d" % b, tag="bank%d" % (2 * b))
-            xt_v = banks.tile([P, 2, T], F32, name="xt_v%d" % b, tag="bank%d" % (2 * b + 1))
-            xt_scalar.append(xt_s)
-            xt_vector.append(xt_v)
+            for u in range(2):
+                xt.append(
+                    banks.tile([P, T], F32, name="xt%d%d" % (b, u), tag="bank%d" % (2 * b + u))
+                )
 
         x_words = x_sb[:].bitcast(F32)
         for b in range(SEQS):
-            for bank in (xt_scalar[b], xt_vector[b]):
-                for u in range(2):
-                    for h in range(HALVES):
-                        nc.tensor.transpose(
-                            bank[:, u, h * P : (h + 1) * P],
-                            x_words[:, b * HALVES + h, u:WORDS:2],
-                            ident_f32[:],
-                        )
+            for u in range(2):
+                for h in range(HALVES):
+                    nc.tensor.transpose(
+                        xt[2 * b + u][:, h * P : (h + 1) * P],
+                        x_words[:, b * HALVES + h, u:WORDS:2],
+                        ident_f32[:],
+                    )
 
-        def channel_plane(bank, t):
-            halves = bank[:].bitcast(BF16).rearrange("p u (c e) -> p u c e", e=2)
-            return halves[:, t // 2, :, t % 2]
+        def channel_plane(b, t):
+            halves = xt[2 * b + t // 2][:].bitcast(BF16).rearrange("p (c e) -> p c e", e=2)
+            return halves[:, :, t % 2]
 
         planes = []
         grouped = []
@@ -114,21 +112,23 @@ def tile_full_tmix_params_pb_s_kernel(
             code_scales.append(keep.tile([P, T], U8, name="code_scales%d" % b, align_bytes=64))
 
         def mix(b):
-            for t in range(PACK):
-                nc.scalar.activation(
-                    out=prev_part[:, b, t, 1:T],
-                    in_=channel_plane(xt_scalar[b], t)[:, 0 : T - 1],
-                    func=ACT.Copy,
-                    scale=mix_prev[:, t : t + 1],
-                )
-                nc.vector.scalar_tensor_tensor(
-                    out=planes[b][:, t, :],
-                    in0=channel_plane(xt_vector[b], t),
-                    scalar=mix_cur[:, t : t + 1],
-                    in1=prev_part[:, b, t, :],
-                    op0=ALU.mult,
-                    op1=ALU.add,
-                )
+            for u in range(2):
+                for t in (2 * u, 2 * u + 1):
+                    nc.scalar.activation(
+                        out=prev_part[:, b, t, 1:T],
+                        in_=channel_plane(b, t)[:, 0 : T - 1],
+                        func=ACT.Copy,
+                        scale=mix_prev[:, t : t + 1],
+                    )
+                for t in (2 * u + 1, 2 * u):
+                    nc.vector.scalar_tensor_tensor(
+                        out=planes[b][:, t, :],
+                        in0=channel_plane(b, t),
+                        scalar=mix_cur[:, t : t + 1],
+                        in1=prev_part[:, b, t, :],
+                        op0=ALU.mult,
+                        op1=ALU.add,
+                    )
 
         def group(b):
             nc.vector.tensor_copy(out=grouped[b][:], in_=planes[b][:].rearrange("p t c -> p c t"))
@@ -176,8 +176,7 @@ def tile_full_tmix_params_pb_s_kernel(
             nc.tensor.transpose(v1t_ps[:, i * P : (i + 1) * P], v1_sb[:, i, :], ident_bf[:])
         group(0)
         v1t = keep.tile([P, TILES * P], BF16)
-        nc.vector.tensor_copy(out=v1t[:], in_=v1t_ps[:])
-        quantise(0)
+        nc.scalar.copy(out=v1t[:], in_=v1t_ps[:])
 
         logit = []
         for j in range(N_TILES):
@@ -188,6 +187,7 @@ def tile_full_tmix_params_pb_s_kernel(
             logit.append(logit_j)
 
         mix(1)
+        quantise(0)
         multiply(0)
 
         gate_t = keep.tile([P, N_TILES, TILES * P], F32)

@@ -21,6 +21,7 @@ HALVES = T // P
 TILES = SEQS * HALVES
 N_TILES = C // P
 WORDS = C // 2
+GPSIMD_TILE = TILES - 1
 
 FLOPS = 2 * SEQS * T * C * C + 2 * SEQS * T * DV * C
 
@@ -202,16 +203,32 @@ def tile_full_tmix_params_pb_s_kernel(
         subtract(1)
         multiply(1)
         subtract(2)
-        subtract(3)
 
-        gate = []
-        for i in range(TILES):
-            gate_i = banks.tile([P, C], F32, name="gate%d" % i, tag="bank%d" % (4 + i))
+        gate = [None] * TILES
+        for i in [GPSIMD_TILE] + list(range(GPSIMD_TILE)):
+            gate[i] = banks.tile([P, C], F32, name="gate%d" % i, tag="bank%d" % (4 + i))
             for j in range(N_TILES):
                 nc.tensor.transpose(
-                    gate_i[:, j * P : (j + 1) * P], gate_t[:, j, i * P : (i + 1) * P], ident_f32[:]
+                    gate[i][:, j * P : (j + 1) * P], gate_t[:, j, i * P : (i + 1) * P], ident_f32[:]
                 )
-            gate.append(gate_i)
+
+        product_sb = keep.tile([P, C], F32)
+        nc.scalar.copy(out=product_sb[:], in_=product[GPSIMD_TILE][:])
+        gate_sb = keep.tile([P, C], F32)
+        nc.scalar.copy(out=gate_sb[:], in_=gate[GPSIMD_TILE][:])
+        nc.gpsimd.tensor_tensor(
+            out=diff[GPSIMD_TILE][:],
+            in0=vf_sb[:, GPSIMD_TILE, :],
+            in1=product_sb[:],
+            op=ALU.subtract,
+        )
+        nc.gpsimd.tensor_tensor(
+            out=step[GPSIMD_TILE][:], in0=diff[GPSIMD_TILE][:], in1=gate_sb[:], op=ALU.mult
+        )
+        nc.gpsimd.tensor_tensor(
+            out=result[GPSIMD_TILE][:], in0=step[GPSIMD_TILE][:], in1=product_sb[:], op=ALU.add
+        )
+        nc.scalar.dma_start(out=out_view[:, GPSIMD_TILE, :], in_=result[GPSIMD_TILE][:])
 
         def finish(i):
             nc.vector.tensor_tensor(
@@ -219,8 +236,8 @@ def tile_full_tmix_params_pb_s_kernel(
             )
             nc.sync.dma_start(out=out_view[:, i, :], in_=result[i][:])
 
-        for i in range(TILES):
+        for i in range(GPSIMD_TILE):
             nc.vector.tensor_tensor(out=step[i][:], in0=diff[i][:], in1=gate[i][:], op=ALU.mult)
             if i > 0:
                 finish(i - 1)
-        finish(TILES - 1)
+        finish(GPSIMD_TILE - 1)

@@ -21,7 +21,8 @@ HALVES = T // P
 TILES = SEQS * HALVES
 N_TILES = C // P
 WORDS = C // 2
-GPSIMD_TILE = TILES - 1
+GPSIMD_TILE = 0
+WARM_TRANSPOSES = 10
 
 FLOPS = 2 * SEQS * T * C * C + 2 * SEQS * T * DV * C
 
@@ -88,6 +89,10 @@ def tile_full_tmix_params_pb_s_kernel(
                     banks.tile([P, T], F32, name="xt%d%d" % (b, u), tag="bank%d" % (2 * b + u))
                 )
 
+        warm_ps = banks.tile([P, C], F32, name="warm_ps", tag="bank7")
+        for r in range(WARM_TRANSPOSES):
+            nc.tensor.transpose(warm_ps[:, (r % 4) * P : (r % 4 + 1) * P], ident_f32[:], ident_f32[:])
+
         x_words = x_sb[:].bitcast(F32)
         for b in range(SEQS):
             for u in range(2):
@@ -112,8 +117,8 @@ def tile_full_tmix_params_pb_s_kernel(
             codes.append(keep.tile([P, T], U32, name="codes%d" % b, align_bytes=64))
             code_scales.append(keep.tile([P, T], U8, name="code_scales%d" % b, align_bytes=64))
 
-        def mix(b):
-            for u in range(2):
+        def mix(b, word_halves=(0, 1)):
+            for u in word_halves:
                 for t in (2 * u, 2 * u + 1):
                     nc.scalar.activation(
                         out=prev_part[:, b, t, 1:T],
@@ -132,7 +137,19 @@ def tile_full_tmix_params_pb_s_kernel(
                     )
 
         def group(b):
-            nc.vector.tensor_copy(out=grouped[b][:], in_=planes[b][:].rearrange("p t c -> p c t"))
+            if b == 2:
+                nc.gpsimd.tensor_scalar(
+                    out=grouped[b][:],
+                    in0=planes[b][:].rearrange("p t c -> p c t"),
+                    scalar1=1.0,
+                    scalar2=0.0,
+                    op0=ALU.mult,
+                    op1=ALU.add,
+                )
+            else:
+                nc.vector.tensor_copy(
+                    out=grouped[b][:], in_=planes[b][:].rearrange("p t c -> p c t")
+                )
 
         def quantise(b):
             nc.vector.quantize_mx(
@@ -187,9 +204,10 @@ def tile_full_tmix_params_pb_s_kernel(
             )
             logit.append(logit_j)
 
-        mix(1)
+        mix(1, (0,))
         quantise(0)
         multiply(0)
+        mix(1, (1,))
 
         gate_t = keep.tile([P, N_TILES, TILES * P], F32)
         for j in range(N_TILES):
@@ -198,19 +216,32 @@ def tile_full_tmix_params_pb_s_kernel(
             )
 
         group(1)
-        subtract(0)
-        quantise(1)
-        subtract(1)
-        multiply(1)
-        subtract(2)
 
         gate = [None] * TILES
-        for i in [GPSIMD_TILE] + list(range(GPSIMD_TILE)):
+
+        def gate_back(i):
             gate[i] = banks.tile([P, C], F32, name="gate%d" % i, tag="bank%d" % (4 + i))
             for j in range(N_TILES):
                 nc.tensor.transpose(
                     gate[i][:, j * P : (j + 1) * P], gate_t[:, j, i * P : (i + 1) * P], ident_f32[:]
                 )
+
+        def scale(i):
+            nc.vector.tensor_tensor(out=step[i][:], in0=diff[i][:], in1=gate[i][:], op=ALU.mult)
+
+        def finish(i):
+            nc.vector.tensor_tensor(
+                out=result[i][:], in0=step[i][:], in1=product[i][:], op=ALU.add
+            )
+            nc.sync.dma_start(out=out_view[:, i, :], in_=result[i][:])
+
+        subtract(1)
+        quantise(1)
+        gate_back(GPSIMD_TILE)
+        gate_back(1)
+        multiply(1)
+        gate_back(2)
+        gate_back(3)
 
         product_sb = keep.tile([P, C], F32)
         nc.scalar.copy(out=product_sb[:], in_=product[GPSIMD_TILE][:])
@@ -230,14 +261,11 @@ def tile_full_tmix_params_pb_s_kernel(
         )
         nc.scalar.dma_start(out=out_view[:, GPSIMD_TILE, :], in_=result[GPSIMD_TILE][:])
 
-        def finish(i):
-            nc.vector.tensor_tensor(
-                out=result[i][:], in0=step[i][:], in1=product[i][:], op=ALU.add
-            )
-            nc.sync.dma_start(out=out_view[:, i, :], in_=result[i][:])
-
-        for i in range(GPSIMD_TILE):
-            nc.vector.tensor_tensor(out=step[i][:], in0=diff[i][:], in1=gate[i][:], op=ALU.mult)
-            if i > 0:
-                finish(i - 1)
-        finish(GPSIMD_TILE - 1)
+        scale(1)
+        finish(1)
+        subtract(2)
+        subtract(3)
+        scale(2)
+        finish(2)
+        scale(3)
+        finish(3)

@@ -256,16 +256,31 @@ def tile_full_tmix_params_pb_s_kernel(
         nc.gpsimd.tensor_tensor(
             out=step[GPSIMD_TILE][:], in0=diff[GPSIMD_TILE][:], in1=gate_sb[:], op=ALU.mult
         )
-        nc.gpsimd.tensor_tensor(
-            out=result[GPSIMD_TILE][:], in0=step[GPSIMD_TILE][:], in1=product_sb[:], op=ALU.add
-        )
-        nc.scalar.dma_start(out=out_view[:, GPSIMD_TILE, :], in_=result[GPSIMD_TILE][:])
+        for half in range(2):
+            cols = slice(half * (C // 2), (half + 1) * (C // 2))
+            nc.gpsimd.tensor_tensor(
+                out=result[GPSIMD_TILE][:, cols],
+                in0=step[GPSIMD_TILE][:, cols],
+                in1=product_sb[:, cols],
+                op=ALU.add,
+            )
+            nc.scalar.dma_start(
+                out=out_view[:, GPSIMD_TILE, cols], in_=result[GPSIMD_TILE][:, cols]
+            )
 
         scale(1)
-        finish(1)
         subtract(2)
-        subtract(3)
+        finish(1)
         scale(2)
+        subtract(3)
         finish(2)
-        scale(3)
-        finish(3)
+        halves = [slice(half * (C // 2), (half + 1) * (C // 2)) for half in range(2)]
+        for cols in halves:
+            nc.vector.tensor_tensor(
+                out=step[3][:, cols], in0=diff[3][:, cols], in1=gate[3][:, cols], op=ALU.mult
+            )
+        for cols in halves:
+            nc.vector.tensor_tensor(
+                out=result[3][:, cols], in0=step[3][:, cols], in1=product[3][:, cols], op=ALU.add
+            )
+            nc.sync.dma_start(out=out_view[:, 3, cols], in_=result[3][:, cols])

@@ -197,12 +197,21 @@ def tile_full_tmix_params_pb_s_kernel(
         nc.scalar.copy(out=v1t[:], in_=v1t_ps[:])
 
         logit = []
-        for j in range(N_TILES):
-            logit_j = banks.tile([P, TILES * P], F32, name="logit%d" % j, tag="bank%d" % (4 + j))
-            nc.tensor.matmul(
-                out=logit_j[:], lhsT=v2_sb[:, j * P : (j + 1) * P], rhs=v1t[:], start=True, stop=True
-            )
-            logit.append(logit_j)
+        for b in range(SEQS):
+            for pair in range(N_TILES // 2):
+                logit_bp = banks.tile(
+                    [P, 2, T], F32, name="logit%d%d" % (b, pair), tag="bank%d" % (4 + 2 * b + pair)
+                )
+                for r in range(2):
+                    j = 2 * pair + r
+                    nc.tensor.matmul(
+                        out=logit_bp[:, r, :],
+                        lhsT=v2_sb[:, j * P : (j + 1) * P],
+                        rhs=v1t[:, b * T : (b + 1) * T],
+                        start=True,
+                        stop=True,
+                    )
+                logit.append(logit_bp)
 
         mix(1, (0,))
         quantise(0)
@@ -210,10 +219,14 @@ def tile_full_tmix_params_pb_s_kernel(
         mix(1, (1,))
 
         gate_t = keep.tile([P, N_TILES, TILES * P], F32)
-        for j in range(N_TILES):
-            nc.scalar.activation(
-                out=gate_t[:, j, :], in_=logit[j][:], func=ACT.Sigmoid, bias=bias[:, j : j + 1]
-            )
+        for b in range(SEQS):
+            for j in range(N_TILES):
+                nc.scalar.activation(
+                    out=gate_t[:, j, b * T : (b + 1) * T],
+                    in_=logit[(N_TILES // 2) * b + j // 2][:, j % 2, :],
+                    func=ACT.Sigmoid,
+                    bias=bias[:, j : j + 1],
+                )
 
         group(1)
 

@@ -252,9 +252,9 @@ def tile_full_tmix_params_pb_s_kernel(
         quantise(1)
         gate_back(GPSIMD_TILE)
         gate_back(1)
-        multiply(1)
         gate_back(2)
         gate_back(3)
+        multiply(1)
 
         product_sb = keep.tile([P, C], F32)
         nc.scalar.copy(out=product_sb[:], in_=product[GPSIMD_TILE][:])

@@ -22,6 +22,7 @@ TILES = SEQS * HALVES
 N_TILES = C // P
 WORDS = C // 2
 GPSIMD_TILE = 0
+GPSIMD_COLS = 384
 WARM_TRANSPOSES = 10
 
 FLOPS = 2 * SEQS * T * C * C + 2 * SEQS * T * DV * C
@@ -256,21 +257,22 @@ def tile_full_tmix_params_pb_s_kernel(
         gate_back(3)
         multiply(1)
 
+        gp = slice(0, GPSIMD_COLS)
         product_sb = keep.tile([P, C], F32)
-        nc.scalar.copy(out=product_sb[:], in_=product[GPSIMD_TILE][:])
+        nc.scalar.copy(out=product_sb[:, gp], in_=product[GPSIMD_TILE][:, gp])
         gate_sb = keep.tile([P, C], F32)
-        nc.scalar.copy(out=gate_sb[:], in_=gate[GPSIMD_TILE][:])
+        nc.scalar.copy(out=gate_sb[:, gp], in_=gate[GPSIMD_TILE][:, gp])
         nc.gpsimd.tensor_tensor(
-            out=diff[GPSIMD_TILE][:],
-            in0=vf_sb[:, GPSIMD_TILE, :],
-            in1=product_sb[:],
+            out=diff[GPSIMD_TILE][:, gp],
+            in0=vf_sb[:, GPSIMD_TILE, gp],
+            in1=product_sb[:, gp],
             op=ALU.subtract,
         )
         nc.gpsimd.tensor_tensor(
-            out=step[GPSIMD_TILE][:], in0=diff[GPSIMD_TILE][:], in1=gate_sb[:], op=ALU.mult
+            out=step[GPSIMD_TILE][:, gp], in0=diff[GPSIMD_TILE][:, gp], in1=gate_sb[:, gp], op=ALU.mult
         )
         for half in range(2):
-            cols = slice(half * (C // 2), (half + 1) * (C // 2))
+            cols = slice(half * (GPSIMD_COLS // 2), (half + 1) * (GPSIMD_COLS // 2))
             nc.gpsimd.tensor_tensor(
                 out=result[GPSIMD_TILE][:, cols],
                 in0=step[GPSIMD_TILE][:, cols],
@@ -281,9 +283,36 @@ def tile_full_tmix_params_pb_s_kernel(
                 out=out_view[:, GPSIMD_TILE, cols], in_=result[GPSIMD_TILE][:, cols]
             )
 
+        rest = slice(GPSIMD_COLS, C)
+        rest_diff = keep.tile([P, C - GPSIMD_COLS], F32)
+        rest_step = keep.tile([P, C - GPSIMD_COLS], F32)
+        rest_result = keep.tile([P, C - GPSIMD_COLS], F32)
+
+        def rest_subtract():
+            nc.vector.tensor_tensor(
+                out=rest_diff[:],
+                in0=vf_sb[:, GPSIMD_TILE, rest],
+                in1=product[GPSIMD_TILE][:, rest],
+                op=ALU.subtract,
+            )
+
+        def rest_scale():
+            nc.vector.tensor_tensor(
+                out=rest_step[:], in0=rest_diff[:], in1=gate[GPSIMD_TILE][:, rest], op=ALU.mult
+            )
+
+        def rest_finish():
+            nc.vector.tensor_tensor(
+                out=rest_result[:], in0=rest_step[:], in1=product[GPSIMD_TILE][:, rest], op=ALU.add
+            )
+            nc.sync.dma_start(out=out_view[:, GPSIMD_TILE, rest], in_=rest_result[:])
+
         scale(1)
-        subtract(2)
+        rest_subtract()
         finish(1)
+        rest_scale()
+        subtract(2)
+        rest_finish()
         scale(2)
         subtract(3)
         finish(2)

@@ -22,7 +22,7 @@ TILES = SEQS * HALVES
 N_TILES = C // P
 WORDS = C // 2
 GPSIMD_TILE = 0
-GPSIMD_COLS = 384
+GPSIMD_COLS = 480
 WARM_TRANSPOSES = 10
 
 FLOPS = 2 * SEQS * T * C * C + 2 * SEQS * T * DV * C

@@ -23,7 +23,6 @@ N_TILES = C // P
 WORDS = C // 2
 GPSIMD_TILE = 0
 GPSIMD_COLS = 480
-WARM_TRANSPOSES = 10
 
 FLOPS = 2 * SEQS * T * C * C + 2 * SEQS * T * DV * C
 
@@ -89,10 +88,6 @@ def tile_full_tmix_params_pb_s_kernel(
                 xt.append(
                     banks.tile([P, T], F32, name="xt%d%d" % (b, u), tag="bank%d" % (2 * b + u))
                 )
-
-        warm_ps = banks.tile([P, C], F32, name="warm_ps", tag="bank7")
-        for r in range(WARM_TRANSPOSES):
-            nc.tensor.transpose(warm_ps[:, (r % 4) * P : (r % 4 + 1) * P], ident_f32[:], ident_f32[:])
 
         x_words = x_sb[:].bitcast(F32)
         for b in range(SEQS):

@@ -46,13 +46,17 @@ def tile_full_tmix_params_pb_s_kernel(
             nc.scalar.dma_start(out=bias[:], in_=v0.rearrange("(j p) -> p j", p=P))
 
         x_sb = keep.tile([P, TILES, C], BF16)
-        for b in range(SEQS):
+        v1_sb = keep.tile([P, TILES, DV], BF16)
+        v2_sb = keep.tile([P, C], BF16)
+
+        def load_x(b):
             tiles_of_b = slice(b * HALVES, (b + 1) * HALVES)
             nc.sync.dma_start(out=x_sb[:, tiles_of_b, :], in_=x_view[:, tiles_of_b, :])
-        v1_sb = keep.tile([P, TILES, DV], BF16)
+
+        load_x(0)
         nc.sync.dma_start(out=v1_sb[:], in_=v1_view)
-        v2_sb = keep.tile([P, C], BF16)
         nc.sync.dma_start(out=v2_sb[:], in_=v2)
+        load_x(1)
         w_words = keep.tile([P, 2 * C], U8, align_bytes=64)
         nc.sync.dma_start(out=w_words[:].bitcast(I32), in_=Wv_words[0].bitcast(I32))
         w_scales = keep.tile([P, C], U8, align_bytes=64)
@@ -90,7 +94,8 @@ def tile_full_tmix_params_pb_s_kernel(
                 )
 
         x_words = x_sb[:].bitcast(F32)
-        for b in range(SEQS):
+
+        def transpose_x(b):
             for u in range(2):
                 for h in range(HALVES):
                     nc.tensor.transpose(
@@ -98,6 +103,12 @@ def tile_full_tmix_params_pb_s_kernel(
                         x_words[:, b * HALVES + h, u:WORDS:2],
                         ident_f32[:],
                     )
+
+        transpose_x(0)
+        v1t_ps = banks.tile([P, TILES * P], BF16, name="v1t_ps", tag="bank4")
+        for i in range(TILES):
+            nc.tensor.transpose(v1t_ps[:, i * P : (i + 1) * P], v1_sb[:, i, :], ident_bf[:])
+        transpose_x(1)
 
         def channel_plane(b, t):
             halves = xt[2 * b + t // 2][:].bitcast(BF16).rearrange("p (c e) -> p c e", e=2)
@@ -185,12 +196,9 @@ def tile_full_tmix_params_pb_s_kernel(
             )
 
         mix(0)
-        v1t_ps = banks.tile([P, TILES * P], BF16, name="v1t_ps", tag="bank4")
-        for i in range(TILES):
-            nc.tensor.transpose(v1t_ps[:, i * P : (i + 1) * P], v1_sb[:, i, :], ident_bf[:])
-        group(0)
         v1t = keep.tile([P, TILES * P], BF16)
         nc.scalar.copy(out=v1t[:], in_=v1t_ps[:])
+        group(0)
 
         logit = []
         for b in range(SEQS):

@@ -22,7 +22,6 @@ TILES = SEQS * HALVES
 N_TILES = C // P
 WORDS = C // 2
 GPSIMD_TILE = 0
-GPSIMD_COLS = 480
 
 FLOPS = 2 * SEQS * T * C * C + 2 * SEQS * T * DV * C
 
@@ -49,14 +48,14 @@ def tile_full_tmix_params_pb_s_kernel(
         v1_sb = keep.tile([P, TILES, DV], BF16)
         v2_sb = keep.tile([P, C], BF16)
 
-        def load_x(b):
-            tiles_of_b = slice(b * HALVES, (b + 1) * HALVES)
-            nc.sync.dma_start(out=x_sb[:, tiles_of_b, :], in_=x_view[:, tiles_of_b, :])
+        def load_x(tiles):
+            nc.sync.dma_start(out=x_sb[:, tiles, :], in_=x_view[:, tiles, :])
 
-        load_x(0)
+        load_x(slice(0, 1))
+        load_x(slice(1, HALVES))
         nc.sync.dma_start(out=v1_sb[:], in_=v1_view)
+        load_x(slice(HALVES, TILES))
         nc.sync.dma_start(out=v2_sb[:], in_=v2)
-        load_x(1)
         w_words = keep.tile([P, 2 * C], U8, align_bytes=64)
         nc.sync.dma_start(out=w_words[:].bitcast(I32), in_=Wv_words[0].bitcast(I32))
         w_scales = keep.tile([P, C], U8, align_bytes=64)
@@ -95,20 +94,22 @@ def tile_full_tmix_params_pb_s_kernel(
 
         x_words = x_sb[:].bitcast(F32)
 
-        def transpose_x(b):
-            for u in range(2):
-                for h in range(HALVES):
-                    nc.tensor.transpose(
-                        xt[2 * b + u][:, h * P : (h + 1) * P],
-                        x_words[:, b * HALVES + h, u:WORDS:2],
-                        ident_f32[:],
-                    )
+        def transpose_x(b, h, u):
+            nc.tensor.transpose(
+                xt[2 * b + u][:, h * P : (h + 1) * P],
+                x_words[:, b * HALVES + h, u:WORDS:2],
+                ident_f32[:],
+            )
 
-        transpose_x(0)
+        for h in range(HALVES):
+            for u in range(2):
+                transpose_x(0, h, u)
         v1t_ps = banks.tile([P, TILES * P], BF16, name="v1t_ps", tag="bank4")
         for i in range(TILES):
             nc.tensor.transpose(v1t_ps[:, i * P : (i + 1) * P], v1_sb[:, i, :], ident_bf[:])
-        transpose_x(1)
+        for u in range(2):
+            for h in range(HALVES):
+                transpose_x(1, h, u)
 
         def channel_plane(b, t):
             halves = xt[2 * b + t // 2][:].bitcast(BF16).rearrange("p (c e) -> p c e", e=2)
@@ -124,39 +125,27 @@ def tile_full_tmix_params_pb_s_kernel(
             codes.append(keep.tile([P, T], U32, name="codes%d" % b, align_bytes=64))
             code_scales.append(keep.tile([P, T], U8, name="code_scales%d" % b, align_bytes=64))
 
-        def mix(b, word_halves=(0, 1)):
-            for u in word_halves:
-                for t in (2 * u, 2 * u + 1):
-                    nc.scalar.activation(
-                        out=prev_part[:, b, t, 1:T],
-                        in_=channel_plane(b, t)[:, 0 : T - 1],
-                        func=ACT.Copy,
-                        scale=mix_prev[:, t : t + 1],
-                    )
-                for t in (2 * u + 1, 2 * u):
-                    nc.vector.scalar_tensor_tensor(
-                        out=planes[b][:, t, :],
-                        in0=channel_plane(b, t),
-                        scalar=mix_cur[:, t : t + 1],
-                        in1=prev_part[:, b, t, :],
-                        op0=ALU.mult,
-                        op1=ALU.add,
-                    )
+        def scale_prev(b, u):
+            for t in (2 * u, 2 * u + 1):
+                nc.scalar.activation(
+                    out=prev_part[:, b, t, 1:T],
+                    in_=channel_plane(b, t)[:, 0 : T - 1],
+                    func=ACT.Copy,
+                    scale=mix_prev[:, t : t + 1],
+                )
 
-        def group(b):
-            if b == 2:
-                nc.gpsimd.tensor_scalar(
-                    out=grouped[b][:],
-                    in0=planes[b][:].rearrange("p t c -> p c t"),
-                    scalar1=1.0,
-                    scalar2=0.0,
-                    op0=ALU.mult,
-                    op1=ALU.add,
-                )
-            else:
-                nc.vector.tensor_copy(
-                    out=grouped[b][:], in_=planes[b][:].rearrange("p t c -> p c t")
-                )
+        def lerp(b, t):
+            nc.vector.scalar_tensor_tensor(
+                out=planes[b][:, t, :],
+                in0=channel_plane(b, t),
+                scalar=mix_cur[:, t : t + 1],
+                in1=prev_part[:, b, t, :],
+                op0=ALU.mult,
+                op1=ALU.add,
+            )
+
+        def group(copy, b, tokens):
+            copy(out=grouped[b][:, tokens, :], in_=planes[b][:, :, tokens].rearrange("p t c -> p c t"))
 
         def quantise(b):
             nc.vector.quantize_mx(
@@ -195,10 +184,13 @@ def tile_full_tmix_params_pb_s_kernel(
                 out=diff[i][:], in0=vf_sb[:, i, :], in1=product[i][:], op=ALU.subtract
             )
 
-        mix(0)
+        for u in range(2):
+            scale_prev(0, u)
+            lerp(0, 2 * u + 1)
+            lerp(0, 2 * u)
         v1t = keep.tile([P, TILES * P], BF16)
         nc.scalar.copy(out=v1t[:], in_=v1t_ps[:])
-        group(0)
+        group(nc.vector.tensor_copy, 0, slice(0, T))
 
         logit = []
         for b in range(SEQS):
@@ -217,22 +209,34 @@ def tile_full_tmix_params_pb_s_kernel(
                     )
                 logit.append(logit_bp)
 
-        mix(1, (0,))
+        scale_prev(1, 0)
+        lerp(1, 1)
         quantise(0)
         multiply(0)
-        mix(1, (1,))
+        lerp(1, 0)
+        scale_prev(1, 1)
+        lerp(1, 3)
+        lerp(1, 2)
 
         gate_t = keep.tile([P, N_TILES, TILES * P], F32)
-        for b in range(SEQS):
-            for j in range(N_TILES):
-                nc.scalar.activation(
-                    out=gate_t[:, j, b * T : (b + 1) * T],
-                    in_=logit[(N_TILES // 2) * b + j // 2][:, j % 2, :],
-                    func=ACT.Sigmoid,
-                    bias=bias[:, j : j + 1],
-                )
 
-        group(1)
+        def sigmoid(b, j):
+            nc.scalar.activation(
+                out=gate_t[:, j, b * T : (b + 1) * T],
+                in_=logit[(N_TILES // 2) * b + j // 2][:, j % 2, :],
+                func=ACT.Sigmoid,
+                bias=bias[:, j : j + 1],
+            )
+
+        for j in range(N_TILES):
+            sigmoid(0, j)
+        sigmoid(1, 0)
+        group(nc.scalar.copy, 1, slice(P, T))
+        group(nc.vector.tensor_copy, 1, slice(0, P))
+        product_sb = keep.tile([P, C], F32)
+        nc.scalar.copy(out=product_sb[:], in_=product[GPSIMD_TILE][:])
+        for j in range(1, N_TILES):
+            sigmoid(1, j)
 
         gate = [None] * TILES
 
@@ -254,28 +258,22 @@ def tile_full_tmix_params_pb_s_kernel(
 
         subtract(1)
         quantise(1)
-        gate_back(GPSIMD_TILE)
         gate_back(1)
+        gate_back(GPSIMD_TILE)
+        multiply(1)
         gate_back(2)
         gate_back(3)
-        multiply(1)
 
-        gp = slice(0, GPSIMD_COLS)
-        product_sb = keep.tile([P, C], F32)
-        nc.scalar.copy(out=product_sb[:, gp], in_=product[GPSIMD_TILE][:, gp])
         gate_sb = keep.tile([P, C], F32)
-        nc.scalar.copy(out=gate_sb[:, gp], in_=gate[GPSIMD_TILE][:, gp])
+        nc.scalar.copy(out=gate_sb[:], in_=gate[GPSIMD_TILE][:])
         nc.gpsimd.tensor_tensor(
-            out=diff[GPSIMD_TILE][:, gp],
-            in0=vf_sb[:, GPSIMD_TILE, gp],
-            in1=product_sb[:, gp],
-            op=ALU.subtract,
+            out=diff[GPSIMD_TILE][:], in0=vf_sb[:, GPSIMD_TILE, :], in1=product_sb[:], op=ALU.subtract
         )
         nc.gpsimd.tensor_tensor(
-            out=step[GPSIMD_TILE][:, gp], in0=diff[GPSIMD_TILE][:, gp], in1=gate_sb[:, gp], op=ALU.mult
+            out=step[GPSIMD_TILE][:], in0=diff[GPSIMD_TILE][:], in1=gate_sb[:], op=ALU.mult
         )
-        for half in range(2):
-            cols = slice(half * (GPSIMD_COLS // 2), (half + 1) * (GPSIMD_COLS // 2))
+        halves = [slice(half * (C // 2), (half + 1) * (C // 2)) for half in range(2)]
+        for cols in halves:
             nc.gpsimd.tensor_tensor(
                 out=result[GPSIMD_TILE][:, cols],
                 in0=step[GPSIMD_TILE][:, cols],
@@ -286,40 +284,12 @@ def tile_full_tmix_params_pb_s_kernel(
                 out=out_view[:, GPSIMD_TILE, cols], in_=result[GPSIMD_TILE][:, cols]
             )
 
-        rest = slice(GPSIMD_COLS, C)
-        rest_diff = keep.tile([P, C - GPSIMD_COLS], F32)
-        rest_step = keep.tile([P, C - GPSIMD_COLS], F32)
-        rest_result = keep.tile([P, C - GPSIMD_COLS], F32)
-
-        def rest_subtract():
-            nc.vector.tensor_tensor(
-                out=rest_diff[:],
-                in0=vf_sb[:, GPSIMD_TILE, rest],
-                in1=product[GPSIMD_TILE][:, rest],
-                op=ALU.subtract,
-            )
-
-        def rest_scale():
-            nc.vector.tensor_tensor(
-                out=rest_step[:], in0=rest_diff[:], in1=gate[GPSIMD_TILE][:, rest], op=ALU.mult
-            )
-
-        def rest_finish():
-            nc.vector.tensor_tensor(
-                out=rest_result[:], in0=rest_step[:], in1=product[GPSIMD_TILE][:, rest], op=ALU.add
-            )
-            nc.sync.dma_start(out=out_view[:, GPSIMD_TILE, rest], in_=rest_result[:])
-
         scale(1)
-        rest_subtract()
-        finish(1)
-        rest_scale()
         subtract(2)
-        rest_finish()
+        finish(1)
         scale(2)
         subtract(3)
         finish(2)
-        halves = [slice(half * (C // 2), (half + 1) * (C // 2)) for half in range(2)]
         for cols in halves:
             nc.vector.tensor_tensor(
                 out=step[3][:, cols], in0=diff[3][:, cols], in1=gate[3][:, cols], op=ALU.mult

@@ -184,35 +184,46 @@ def tile_full_tmix_params_pb_s_kernel(
                 out=diff[i][:], in0=vf_sb[:, i, :], in1=product[i][:], op=ALU.subtract
             )
 
-        for u in range(2):
-            scale_prev(0, u)
-            lerp(0, 2 * u + 1)
-            lerp(0, 2 * u)
+        scale_prev(0, 0)
+        for t in (2, 3):
+            nc.vector.tensor_scalar(
+                out=prev_part[:, 0, t, 1:T],
+                in0=channel_plane(0, t)[:, 0 : T - 1],
+                scalar1=mix_prev[:, t : t + 1],
+                scalar2=None,
+                op0=ALU.mult,
+            )
+        for t in (2, 3, 1, 0):
+            lerp(0, t)
         v1t = keep.tile([P, TILES * P], BF16)
         nc.scalar.copy(out=v1t[:], in_=v1t_ps[:])
         group(nc.vector.tensor_copy, 0, slice(0, T))
 
-        logit = []
-        for b in range(SEQS):
-            for pair in range(N_TILES // 2):
-                logit_bp = banks.tile(
-                    [P, 2, T], F32, name="logit%d%d" % (b, pair), tag="bank%d" % (4 + 2 * b + pair)
+        pairs = N_TILES // 2
+        logit = [None] * (SEQS * pairs)
+
+        def make_logits(b, pair):
+            bp = b * pairs + pair
+            logit[bp] = banks.tile([P, 2, T], F32, name="logit%d" % bp, tag="bank%d" % (4 + bp))
+            for r in range(2):
+                j = 2 * pair + r
+                nc.tensor.matmul(
+                    out=logit[bp][:, r, :],
+                    lhsT=v2_sb[:, j * P : (j + 1) * P],
+                    rhs=v1t[:, b * T : (b + 1) * T],
+                    start=True,
+                    stop=True,
                 )
-                for r in range(2):
-                    j = 2 * pair + r
-                    nc.tensor.matmul(
-                        out=logit_bp[:, r, :],
-                        lhsT=v2_sb[:, j * P : (j + 1) * P],
-                        rhs=v1t[:, b * T : (b + 1) * T],
-                        start=True,
-                        stop=True,
-                    )
-                logit.append(logit_bp)
+
+        make_logits(0, 0)
+        make_logits(0, 1)
+        make_logits(1, 0)
 
         scale_prev(1, 0)
         lerp(1, 1)
         quantise(0)
         multiply(0)
+        make_logits(1, 1)
         lerp(1, 0)
         scale_prev(1, 1)
         lerp(1, 3)
@@ -223,7 +234,7 @@ def tile_full_tmix_params_pb_s_kernel(
         def sigmoid(b, j):
             nc.scalar.activation(
                 out=gate_t[:, j, b * T : (b + 1) * T],
-                in_=logit[(N_TILES // 2) * b + j // 2][:, j % 2, :],
+                in_=logit[pairs * b + j // 2][:, j % 2, :],
                 func=ACT.Sigmoid,
                 bias=bias[:, j : j + 1],
             )

@@ -102,7 +102,7 @@ def tile_full_tmix_params_pb_s_kernel(
             )
 
         for h in range(HALVES):
-            for u in range(2):
+            for u in (1, 0):
                 transpose_x(0, h, u)
         v1t_ps = banks.tile([P, TILES * P], BF16, name="v1t_ps", tag="bank4")
         for i in range(TILES):

@@ -32,7 +32,7 @@ def tile_full_tmix_params_pb_s_kernel(
     nc = tc.nc
     x_view = x.flatten_outer_dims().rearrange("(i p) c -> p i c", p=P)
     vf_view = v_first.flatten_outer_dims().rearrange("(i p) c -> p i c", p=P)
-    v1_view = xv_v1.flatten_outer_dims().rearrange("(i p) d -> p i d", p=P)
+    v1_view = xv_v1.flatten_outer_dims().rearrange("(p i) d -> p i d", p=P)
     out_view = out.flatten_outer_dims().rearrange("(i p) n -> p i n", p=P)
 
     with tc.tile_pool(name="keep", bufs=1) as keep, tc.psum_pool(
@@ -84,6 +84,9 @@ def tile_full_tmix_params_pb_s_kernel(
         nc.vector.tensor_scalar(
             out=mix_cur[:], in0=mix_bf[:], scalar1=-1.0, scalar2=1.0, op0=ALU.mult, op1=ALU.add
         )
+
+        v0_col = keep.tile([P, N_TILES], F32)
+        nc.gpsimd.tensor_copy(out=v0_col[:], in_=bias[:])
 
         xt = []
         for b in range(SEQS):
@@ -196,34 +199,36 @@ def tile_full_tmix_params_pb_s_kernel(
         for t in (2, 3, 1, 0):
             lerp(0, t)
         v1t = keep.tile([P, TILES * P], BF16)
-        nc.scalar.copy(out=v1t[:], in_=v1t_ps[:])
+        nc.scalar.copy(
+            out=v1t[:].rearrange("p (c i) -> p c i", i=TILES),
+            in_=v1t_ps[:].rearrange("p (i c) -> p c i", i=TILES),
+        )
         group(nc.vector.tensor_copy, 0, slice(0, T))
 
-        pairs = N_TILES // 2
-        logit = [None] * (SEQS * pairs)
+        def channel_logit(out, j, tokens):
+            nc.tensor.matmul(
+                out=out, lhsT=v2_sb[:, j * P : (j + 1) * P], rhs=v1t[:, tokens], start=True, stop=True
+            )
 
-        def make_logits(b, pair):
-            bp = b * pairs + pair
-            logit[bp] = banks.tile([P, 2, T], F32, name="logit%d" % bp, tag="bank%d" % (4 + bp))
+        logit_1 = banks.tile([P, N_TILES, P], F32, name="logit_1", tag="bank5")
+        for j in range(N_TILES):
+            channel_logit(logit_1[:, j, :], j, slice(P, 2 * P))
+        logit_23 = []
+        for pair in range(N_TILES // 2):
+            logit_23.append(
+                banks.tile([P, 2, T], F32, name="logit_23_%d" % pair, tag="bank%d" % (6 + pair))
+            )
+
+        def logits_23(pair):
             for r in range(2):
-                j = 2 * pair + r
-                nc.tensor.matmul(
-                    out=logit[bp][:, r, :],
-                    lhsT=v2_sb[:, j * P : (j + 1) * P],
-                    rhs=v1t[:, b * T : (b + 1) * T],
-                    start=True,
-                    stop=True,
-                )
+                channel_logit(logit_23[pair][:, r, :], 2 * pair + r, slice(T, 2 * T))
 
-        make_logits(0, 0)
-        make_logits(0, 1)
-        make_logits(1, 0)
+        logits_23(0)
 
         scale_prev(1, 0)
         lerp(1, 1)
         quantise(0)
         multiply(0)
-        make_logits(1, 1)
         lerp(1, 0)
         scale_prev(1, 1)
         lerp(1, 3)
@@ -231,28 +236,18 @@ def tile_full_tmix_params_pb_s_kernel(
 
         gate_t = keep.tile([P, N_TILES, TILES * P], F32)
 
-        def sigmoid(b, j):
+        def sigmoid(logits, j, tokens):
             nc.scalar.activation(
-                out=gate_t[:, j, b * T : (b + 1) * T],
-                in_=logit[pairs * b + j // 2][:, j % 2, :],
-                func=ACT.Sigmoid,
-                bias=bias[:, j : j + 1],
+                out=gate_t[:, j, tokens], in_=logits, func=ACT.Sigmoid, bias=bias[:, j : j + 1]
             )
 
-        for j in range(N_TILES):
-            sigmoid(0, j)
-        sigmoid(1, 0)
-        group(nc.scalar.copy, 1, slice(P, T))
-        group(nc.vector.tensor_copy, 1, slice(0, P))
-        product_sb = keep.tile([P, C], F32)
-        nc.scalar.copy(out=product_sb[:], in_=product[GPSIMD_TILE][:])
-        for j in range(1, N_TILES):
-            sigmoid(1, j)
+        def sigmoid_23(j):
+            sigmoid(logit_23[j // 2][:, j % 2, :], j, slice(T, 2 * T))
 
         gate = [None] * TILES
 
-        def gate_back(i):
-            gate[i] = banks.tile([P, C], F32, name="gate%d" % i, tag="bank%d" % (4 + i))
+        def gate_back(i, bank):
+            gate[i] = banks.tile([P, C], F32, name="gate%d" % i, tag="bank%d" % bank)
             for j in range(N_TILES):
                 nc.tensor.transpose(
                     gate[i][:, j * P : (j + 1) * P], gate_t[:, j, i * P : (i + 1) * P], ident_f32[:]
@@ -267,16 +262,39 @@ def tile_full_tmix_params_pb_s_kernel(
             )
             nc.sync.dma_start(out=out_view[:, i, :], in_=result[i][:])
 
+        for j in range(N_TILES):
+            sigmoid(logit_1[:, j, :], j, slice(P, 2 * P))
+        gate_back(1, 4)
+        logits_23(1)
+        sigmoid_23(0)
+        sigmoid_23(1)
+        group(nc.scalar.copy, 1, slice(P, T))
+        group(nc.vector.tensor_copy, 1, slice(0, P))
         subtract(1)
         quantise(1)
-        gate_back(1)
-        gate_back(GPSIMD_TILE)
+        product_sb = keep.tile([P, C], F32)
+        nc.scalar.copy(out=product_sb[:], in_=product[GPSIMD_TILE][:])
+        logit_0 = banks.tile([P, C], F32, name="logit_0", tag="bank5")
+        nc.tensor.matmul(
+            out=logit_0[:], lhsT=v1t[:, 0:P], rhs=v2_sb[:], start=True, stop=False
+        )
+        for j in range(N_TILES):
+            nc.tensor.matmul(
+                out=logit_0[:, j * P : (j + 1) * P],
+                lhsT=v0_col[:, j : j + 1].to_broadcast([P, P]),
+                rhs=ident_f32[:],
+                start=False,
+                stop=j == N_TILES - 1,
+                is_transpose=True,
+            )
         multiply(1)
-        gate_back(2)
-        gate_back(3)
-
         gate_sb = keep.tile([P, C], F32)
-        nc.scalar.copy(out=gate_sb[:], in_=gate[GPSIMD_TILE][:])
+        nc.scalar.activation(out=gate_sb[:], in_=logit_0[:], func=ACT.Sigmoid)
+        for j in (2, 3):
+            sigmoid_23(j)
+        gate_back(2, 6)
+        gate_back(3, 7)
+
         nc.gpsimd.tensor_tensor(
             out=diff[GPSIMD_TILE][:], in0=vf_sb[:, GPSIMD_TILE, :], in1=product_sb[:], op=ALU.subtract
         )

@@ -159,8 +159,8 @@ def tile_full_tmix_params_pb_s_kernel(
 
         product = [None] * TILES
 
-        def multiply(b):
-            for h in range(HALVES):
+        def multiply(b, order):
+            for h in order:
                 i = b * HALVES + h
                 product[i] = banks.tile([P, C], F32, name="product%d" % i, tag="bank%d" % i)
                 tokens = slice(h * P, (h + 1) * P)
@@ -205,12 +205,25 @@ def tile_full_tmix_params_pb_s_kernel(
         )
         group(nc.vector.tensor_copy, 0, slice(0, T))
 
+        logit_0 = banks.tile([P, C], F32, name="logit_0", tag="bank5")
+        for j in range(N_TILES):
+            nc.tensor.matmul(
+                out=logit_0[:, j * P : (j + 1) * P],
+                lhsT=v0_col[:, j : j + 1].to_broadcast([P, P]),
+                rhs=ident_f32[:],
+                start=j == 0,
+                stop=False,
+                is_transpose=True,
+            )
+        nc.tensor.matmul(
+            out=logit_0[:], lhsT=v1t[:, 0:P], rhs=v2_sb[:], start=False, stop=True
+        )
         def channel_logit(out, j, tokens):
             nc.tensor.matmul(
                 out=out, lhsT=v2_sb[:, j * P : (j + 1) * P], rhs=v1t[:, tokens], start=True, stop=True
             )
 
-        logit_1 = banks.tile([P, N_TILES, P], F32, name="logit_1", tag="bank5")
+        logit_1 = banks.tile([P, N_TILES, P], F32, name="logit_1", tag="bank4")
         for j in range(N_TILES):
             channel_logit(logit_1[:, j, :], j, slice(P, 2 * P))
         logit_23 = []
@@ -219,16 +232,10 @@ def tile_full_tmix_params_pb_s_kernel(
                 banks.tile([P, 2, T], F32, name="logit_23_%d" % pair, tag="bank%d" % (6 + pair))
             )
 
-        def logits_23(pair):
-            for r in range(2):
-                channel_logit(logit_23[pair][:, r, :], 2 * pair + r, slice(T, 2 * T))
-
-        logits_23(0)
-
         scale_prev(1, 0)
         lerp(1, 1)
         quantise(0)
-        multiply(0)
+        multiply(0, (1, 0))
         lerp(1, 0)
         scale_prev(1, 1)
         lerp(1, 3)
@@ -262,51 +269,45 @@ def tile_full_tmix_params_pb_s_kernel(
             )
             nc.sync.dma_start(out=out_view[:, i, :], in_=result[i][:])
 
+        halves = [slice(half * (C // 2), (half + 1) * (C // 2)) for half in range(2)]
+        gate_sb = keep.tile([P, C], F32)
+        nc.scalar.activation(out=gate_sb[:], in_=logit_0[:], func=ACT.Sigmoid)
+        kept = keep.tile([P, C], F32)
+        for cols in halves:
+            nc.gpsimd.tensor_tensor(
+                out=kept[:, cols], in0=vf_sb[:, GPSIMD_TILE, cols], in1=gate_sb[:, cols], op=ALU.mult
+            )
         for j in range(N_TILES):
             sigmoid(logit_1[:, j, :], j, slice(P, 2 * P))
         gate_back(1, 4)
-        logits_23(1)
-        sigmoid_23(0)
-        sigmoid_23(1)
+        rest_sb = keep.tile([P, C], F32)
+        nc.scalar.activation(out=rest_sb[:], in_=logit_0[:], func=ACT.Sigmoid, scale=-1.0)
+        for pair in range(N_TILES // 2):
+            for r in range(2):
+                j = 2 * pair + r
+                channel_logit(logit_23[pair][:, r, :], j, slice(T, 2 * T))
         group(nc.scalar.copy, 1, slice(P, T))
         group(nc.vector.tensor_copy, 1, slice(0, P))
         subtract(1)
         quantise(1)
+        multiply(1, (0, 1))
         product_sb = keep.tile([P, C], F32)
         nc.scalar.copy(out=product_sb[:], in_=product[GPSIMD_TILE][:])
-        logit_0 = banks.tile([P, C], F32, name="logit_0", tag="bank5")
-        nc.tensor.matmul(
-            out=logit_0[:], lhsT=v1t[:, 0:P], rhs=v2_sb[:], start=True, stop=False
-        )
         for j in range(N_TILES):
-            nc.tensor.matmul(
-                out=logit_0[:, j * P : (j + 1) * P],
-                lhsT=v0_col[:, j : j + 1].to_broadcast([P, P]),
-                rhs=ident_f32[:],
-                start=False,
-                stop=j == N_TILES - 1,
-                is_transpose=True,
-            )
-        multiply(1)
-        gate_sb = keep.tile([P, C], F32)
-        nc.scalar.activation(out=gate_sb[:], in_=logit_0[:], func=ACT.Sigmoid)
-        for j in (2, 3):
             sigmoid_23(j)
-        gate_back(2, 6)
-        gate_back(3, 7)
-
-        nc.gpsimd.tensor_tensor(
-            out=diff[GPSIMD_TILE][:], in0=vf_sb[:, GPSIMD_TILE, :], in1=product_sb[:], op=ALU.subtract
-        )
-        nc.gpsimd.tensor_tensor(
-            out=step[GPSIMD_TILE][:], in0=diff[GPSIMD_TILE][:], in1=gate_sb[:], op=ALU.mult
-        )
-        halves = [slice(half * (C // 2), (half + 1) * (C // 2)) for half in range(2)]
+        gate_back(2, 5)
+        gate_back(3, 6)
         for cols in halves:
+            nc.gpsimd.tensor_tensor(
+                out=step[GPSIMD_TILE][:, cols],
+                in0=product_sb[:, cols],
+                in1=rest_sb[:, cols],
+                op=ALU.mult,
+            )
             nc.gpsimd.tensor_tensor(
                 out=result[GPSIMD_TILE][:, cols],
                 in0=step[GPSIMD_TILE][:, cols],
-                in1=product_sb[:, cols],
+                in1=kept[:, cols],
                 op=ALU.add,
             )
             nc.scalar.dma_start(

@@ -271,17 +271,25 @@ def tile_full_tmix_params_pb_s_kernel(
 
         halves = [slice(half * (C // 2), (half + 1) * (C // 2)) for half in range(2)]
         gate_sb = keep.tile([P, C], F32)
-        nc.scalar.activation(out=gate_sb[:], in_=logit_0[:], func=ACT.Sigmoid)
-        kept = keep.tile([P, C], F32)
-        for cols in halves:
-            nc.gpsimd.tensor_tensor(
-                out=kept[:, cols], in0=vf_sb[:, GPSIMD_TILE, cols], in1=gate_sb[:, cols], op=ALU.mult
-            )
+
+        def gpsimd_gate(cols):
+            nc.scalar.activation(out=gate_sb[:, cols], in_=logit_0[:, cols], func=ACT.Sigmoid)
+
+        def gpsimd_step(out, in0, in1, op):
+            nc.gpsimd.tensor_tensor(out=out, in0=in0, in1=in1, op=op)
+
+        first, second = halves
+        vf_gp = vf_sb[:, GPSIMD_TILE, :]
+        gpsimd_gate(second)
+        kept = keep.tile([P, C // 2], F32)
+        gpsimd_step(kept[:], vf_gp[:, second], gate_sb[:, second], ALU.mult)
         for j in range(N_TILES):
             sigmoid(logit_1[:, j, :], j, slice(P, 2 * P))
         gate_back(1, 4)
-        rest_sb = keep.tile([P, C], F32)
-        nc.scalar.activation(out=rest_sb[:], in_=logit_0[:], func=ACT.Sigmoid, scale=-1.0)
+        rest_sb = keep.tile([P, C // 2], F32)
+        nc.scalar.activation(
+            out=rest_sb[:], in_=logit_0[:, second], func=ACT.Sigmoid, scale=-1.0
+        )
         for pair in range(N_TILES // 2):
             for r in range(2):
                 j = 2 * pair + r
@@ -295,24 +303,23 @@ def tile_full_tmix_params_pb_s_kernel(
         nc.scalar.copy(out=product_sb[:], in_=product[GPSIMD_TILE][:])
         for j in range(N_TILES):
             sigmoid_23(j)
-        gate_back(2, 5)
-        gate_back(3, 6)
-        for cols in halves:
-            nc.gpsimd.tensor_tensor(
-                out=step[GPSIMD_TILE][:, cols],
-                in0=product_sb[:, cols],
-                in1=rest_sb[:, cols],
-                op=ALU.mult,
-            )
-            nc.gpsimd.tensor_tensor(
-                out=result[GPSIMD_TILE][:, cols],
-                in0=step[GPSIMD_TILE][:, cols],
-                in1=kept[:, cols],
-                op=ALU.add,
-            )
+        gpsimd_gate(first)
+        gate_back(2, 6)
+        gate_back(3, 7)
+
+        def gpsimd_store(cols):
             nc.scalar.dma_start(
                 out=out_view[:, GPSIMD_TILE, cols], in_=result[GPSIMD_TILE][:, cols]
             )
+
+        gp_diff, gp_step, gp_result = diff[GPSIMD_TILE], step[GPSIMD_TILE], result[GPSIMD_TILE]
+        gpsimd_step(gp_step[:, second], product_sb[:, second], rest_sb[:], ALU.mult)
+        gpsimd_step(gp_diff[:, first], vf_gp[:, first], product_sb[:, first], ALU.subtract)
+        gpsimd_step(gp_result[:, second], gp_step[:, second], kept[:], ALU.add)
+        gpsimd_store(second)
+        gpsimd_step(gp_step[:, first], gp_diff[:, first], gate_sb[:, first], ALU.mult)
+        gpsimd_step(gp_result[:, first], gp_step[:, first], product_sb[:, first], ALU.add)
+        gpsimd_store(first)
 
         scale(1)
         subtract(2)

import concourse.mybir as mybir
from concourse.masks import make_identity

F32 = mybir.dt.float32
BF16 = mybir.dt.bfloat16
I32 = mybir.dt.int32
U32 = mybir.dt.uint32
U8 = mybir.dt.uint8
FP8X4 = mybir.dt.float8_e4m3fn_x4
FP4X4 = mybir.dt.float4_e2m1fn_x4
ALU = mybir.AluOpType
ACT = mybir.ActivationFunctionType

P = 128
PACK = 4
SEQS = 2
T = 256
C = 512
DV = 128
HALVES = T // P
TILES = SEQS * HALVES
N_TILES = C // P
WORDS = C // 2
GPSIMD_TILE = 0

FLOPS = 2 * SEQS * T * C * C + 2 * SEQS * T * DV * C


def tile_full_tmix_params_pb_s_kernel(
    tc, x, v_first, x_v, Wv_words, Wv_scales, v0, xv_v1, v2, out
):
    nc = tc.nc
    x_view = x.flatten_outer_dims().rearrange("(i p) c -> p i c", p=P)
    vf_view = v_first.flatten_outer_dims().rearrange("(i p) c -> p i c", p=P)
    v1_view = xv_v1.flatten_outer_dims().rearrange("(p i) d -> p i d", p=P)
    out_view = out.flatten_outer_dims().rearrange("(i p) n -> p i n", p=P)

    with tc.tile_pool(name="keep", bufs=1) as keep, tc.psum_pool(
        name="banks", bufs=1
    ) as banks, tc.manual_schedule():
        mix_bf = keep.tile([P, PACK], BF16)
        nc.scalar.dma_start(out=mix_bf[:], in_=x_v.rearrange("(p t) -> p t", t=PACK))
        bias = keep.tile([P, N_TILES], BF16)
        with nc.allow_non_contiguous_dma(reason="512 values, one to a partition and column"):
            nc.scalar.dma_start(out=bias[:], in_=v0.rearrange("(j p) -> p j", p=P))

        x_sb = keep.tile([P, TILES, C], BF16)
        v1_sb = keep.tile([P, TILES, DV], BF16)
        v2_sb = keep.tile([P, C], BF16)

        def load_x(tiles):
            nc.sync.dma_start(out=x_sb[:, tiles, :], in_=x_view[:, tiles, :])

        load_x(slice(0, 1))
        load_x(slice(1, HALVES))
        nc.sync.dma_start(out=v1_sb[:], in_=v1_view)
        load_x(slice(HALVES, TILES))
        nc.sync.dma_start(out=v2_sb[:], in_=v2)
        w_words = keep.tile([P, 2 * C], U8, align_bytes=64)
        nc.sync.dma_start(out=w_words[:].bitcast(I32), in_=Wv_words[0].bitcast(I32))
        w_scales = keep.tile([P, C], U8, align_bytes=64)
        nc.vector.memset(w_scales[:].bitcast(I32), 0)
        for quadrant in range(4):
            nc.sync.dma_start(
                out=w_scales[32 * quadrant : 32 * quadrant + 4, :].bitcast(I32),
                in_=Wv_scales[0, 4 * quadrant : 4 * quadrant + 4, :].bitcast(I32),
            )
        vf_sb = keep.tile([P, TILES, C], BF16)
        nc.sync.dma_start(out=vf_sb[:], in_=vf_view)

        ident_f32 = keep.tile([P, P], F32)
        make_identity(nc, ident_f32[:])
        ident_bf = keep.tile([P, P], BF16)
        make_identity(nc, ident_bf[:])
        prev_part = keep.tile([P, SEQS, PACK, T], F32)
        nc.gpsimd.memset(prev_part[:, :, :, 0:8], 0.0)
        warm_in = keep.tile([P, 1], F32)
        nc.vector.memset(warm_in[:], 0.0)
        warm_out = keep.tile([P, 1], F32)
        nc.scalar.activation(out=warm_out[:], in_=warm_in[:], func=ACT.Sigmoid)
        mix_prev = keep.tile([P, PACK], F32)
        nc.vector.tensor_copy(out=mix_prev[:], in_=mix_bf[:])
        mix_cur = keep.tile([P, PACK], F32)
        nc.vector.tensor_scalar(
            out=mix_cur[:], in0=mix_bf[:], scalar1=-1.0, scalar2=1.0, op0=ALU.mult, op1=ALU.add
        )

        v0_col = keep.tile([P, N_TILES], F32)
        nc.gpsimd.tensor_copy(out=v0_col[:], in_=bias[:])

        xt = []
        for b in range(SEQS):
            for u in range(2):
                xt.append(
                    banks.tile([P, T], F32, name="xt%d%d" % (b, u), tag="bank%d" % (2 * b + u))
                )

        x_words = x_sb[:].bitcast(F32)

        def transpose_x(b, h, u):
            nc.tensor.transpose(
                xt[2 * b + u][:, h * P : (h + 1) * P],
                x_words[:, b * HALVES + h, u:WORDS:2],
                ident_f32[:],
            )

        for h in range(HALVES):
            for u in (1, 0):
                transpose_x(0, h, u)
        v1t_ps = banks.tile([P, TILES * P], BF16, name="v1t_ps", tag="bank4")
        for i in range(TILES):
            nc.tensor.transpose(v1t_ps[:, i * P : (i + 1) * P], v1_sb[:, i, :], ident_bf[:])
        for u in range(2):
            for h in range(HALVES):
                transpose_x(1, h, u)

        def channel_plane(b, t):
            halves = xt[2 * b + t // 2][:].bitcast(BF16).rearrange("p (c e) -> p c e", e=2)
            return halves[:, :, t % 2]

        planes = []
        grouped = []
        codes = []
        code_scales = []
        for b in range(SEQS):
            planes.append(keep.tile([P, PACK, T], BF16, name="planes%d" % b))
            grouped.append(keep.tile([P, T, PACK], BF16, name="grouped%d" % b, align_bytes=64))
            codes.append(keep.tile([P, T], U32, name="codes%d" % b, align_bytes=64))
            code_scales.append(keep.tile([P, T], U8, name="code_scales%d" % b, align_bytes=64))

        def scale_prev(b, u):
            for t in (2 * u, 2 * u + 1):
                nc.scalar.activation(
                    out=prev_part[:, b, t, 1:T],
                    in_=channel_plane(b, t)[:, 0 : T - 1],
                    func=ACT.Copy,
                    scale=mix_prev[:, t : t + 1],
                )

        def lerp(b, t):
            nc.vector.scalar_tensor_tensor(
                out=planes[b][:, t, :],
                in0=channel_plane(b, t),
                scalar=mix_cur[:, t : t + 1],
                in1=prev_part[:, b, t, :],
                op0=ALU.mult,
                op1=ALU.add,
            )

        def group(copy, b, tokens):
            copy(out=grouped[b][:, tokens, :], in_=planes[b][:, :, tokens].rearrange("p t c -> p c t"))

        def quantise(b):
            nc.vector.quantize_mx(
                out=codes[b][:].bitcast(FP8X4),
                scales=code_scales[b][:],
                in_=grouped[b][:].rearrange("p c t -> p (c t)"),
            )

        product = [None] * TILES

        def multiply(b, order):
            for h in order:
                i = b * HALVES + h
                product[i] = banks.tile([P, C], F32, name="product%d" % i, tag="bank%d" % i)
                tokens = slice(h * P, (h + 1) * P)
                nc.tensor.matmul_mx(
                    out=product[i][:],
                    lhsT=codes[b][:, tokens].bitcast(FP8X4),
                    lhsT_scale=code_scales[b][:, tokens],
                    rhs=w_words[:].bitcast(FP4X4),
                    rhs_scale=w_scales[:],
                    start=True,
                    stop=True,
                )

        diff = []
        step = []
        result = []
        for i in range(TILES):
            diff.append(keep.tile([P, C], F32, name="diff%d" % i))
            step.append(keep.tile([P, C], F32, name="step%d" % i))
            result.append(keep.tile([P, C], F32, name="result%d" % i))

        def subtract(i):
            nc.vector.tensor_tensor(
                out=diff[i][:], in0=vf_sb[:, i, :], in1=product[i][:], op=ALU.subtract
            )

        scale_prev(0, 0)
        for t in (2, 3):
            nc.vector.tensor_scalar(
                out=prev_part[:, 0, t, 1:T],
                in0=channel_plane(0, t)[:, 0 : T - 1],
                scalar1=mix_prev[:, t : t + 1],
                scalar2=None,
                op0=ALU.mult,
            )
        for t in (2, 3, 1, 0):
            lerp(0, t)
        v1t = keep.tile([P, TILES * P], BF16)
        nc.scalar.copy(
            out=v1t[:].rearrange("p (c i) -> p c i", i=TILES),
            in_=v1t_ps[:].rearrange("p (i c) -> p c i", i=TILES),
        )
        group(nc.vector.tensor_copy, 0, slice(0, T))

        logit_0 = banks.tile([P, C], F32, name="logit_0", tag="bank5")
        for j in range(N_TILES):
            nc.tensor.matmul(
                out=logit_0[:, j * P : (j + 1) * P],
                lhsT=v0_col[:, j : j + 1].to_broadcast([P, P]),
                rhs=ident_f32[:],
                start=j == 0,
                stop=False,
                is_transpose=True,
            )
        nc.tensor.matmul(
            out=logit_0[:], lhsT=v1t[:, 0:P], rhs=v2_sb[:], start=False, stop=True
        )
        def channel_logit(out, j, tokens):
            nc.tensor.matmul(
                out=out, lhsT=v2_sb[:, j * P : (j + 1) * P], rhs=v1t[:, tokens], start=True, stop=True
            )

        logit_1 = banks.tile([P, N_TILES, P], F32, name="logit_1", tag="bank4")
        for j in range(N_TILES):
            channel_logit(logit_1[:, j, :], j, slice(P, 2 * P))
        logit_23 = []
        for pair in range(N_TILES // 2):
            logit_23.append(
                banks.tile([P, 2, T], F32, name="logit_23_%d" % pair, tag="bank%d" % (6 + pair))
            )

        scale_prev(1, 0)
        lerp(1, 1)
        quantise(0)
        multiply(0, (1, 0))
        lerp(1, 0)
        scale_prev(1, 1)
        lerp(1, 3)
        lerp(1, 2)

        gate_t = keep.tile([P, N_TILES, TILES * P], F32)

        def sigmoid(logits, j, tokens):
            nc.scalar.activation(
                out=gate_t[:, j, tokens], in_=logits, func=ACT.Sigmoid, bias=bias[:, j : j + 1]
            )

        def sigmoid_23(j):
            sigmoid(logit_23[j // 2][:, j % 2, :], j, slice(T, 2 * T))

        gate = [None] * TILES

        def gate_back(i, bank):
            gate[i] = banks.tile([P, C], F32, name="gate%d" % i, tag="bank%d" % bank)
            for j in range(N_TILES):
                nc.tensor.transpose(
                    gate[i][:, j * P : (j + 1) * P], gate_t[:, j, i * P : (i + 1) * P], ident_f32[:]
                )

        def scale(i):
            nc.vector.tensor_tensor(out=step[i][:], in0=diff[i][:], in1=gate[i][:], op=ALU.mult)

        def finish(i):
            nc.vector.tensor_tensor(
                out=result[i][:], in0=step[i][:], in1=product[i][:], op=ALU.add
            )
            nc.sync.dma_start(out=out_view[:, i, :], in_=result[i][:])

        halves = [slice(half * (C // 2), (half + 1) * (C // 2)) for half in range(2)]
        gate_sb = keep.tile([P, C], F32)

        def gpsimd_gate(cols):
            nc.scalar.activation(out=gate_sb[:, cols], in_=logit_0[:, cols], func=ACT.Sigmoid)

        def gpsimd_step(out, in0, in1, op):
            nc.gpsimd.tensor_tensor(out=out, in0=in0, in1=in1, op=op)

        first, second = halves
        vf_gp = vf_sb[:, GPSIMD_TILE, :]
        gpsimd_gate(second)
        kept = keep.tile([P, C // 2], F32)
        gpsimd_step(kept[:], vf_gp[:, second], gate_sb[:, second], ALU.mult)
        for j in range(N_TILES):
            sigmoid(logit_1[:, j, :], j, slice(P, 2 * P))
        gate_back(1, 4)
        rest_sb = keep.tile([P, C // 2], F32)
        nc.scalar.activation(
            out=rest_sb[:], in_=logit_0[:, second], func=ACT.Sigmoid, scale=-1.0
        )
        for pair in range(N_TILES // 2):
            for r in range(2):
                j = 2 * pair + r
                channel_logit(logit_23[pair][:, r, :], j, slice(T, 2 * T))
        group(nc.scalar.copy, 1, slice(P, T))
        group(nc.vector.tensor_copy, 1, slice(0, P))
        subtract(1)
        quantise(1)
        multiply(1, (0, 1))
        product_sb = keep.tile([P, C], F32)
        nc.scalar.copy(out=product_sb[:], in_=product[GPSIMD_TILE][:])
        for j in range(N_TILES):
            sigmoid_23(j)
        gpsimd_gate(first)
        gate_back(2, 6)
        gate_back(3, 7)

        def gpsimd_store(cols):
            nc.scalar.dma_start(
                out=out_view[:, GPSIMD_TILE, cols], in_=result[GPSIMD_TILE][:, cols]
            )

        gp_diff, gp_step, gp_result = diff[GPSIMD_TILE], step[GPSIMD_TILE], result[GPSIMD_TILE]
        gpsimd_step(gp_step[:, second], product_sb[:, second], rest_sb[:], ALU.mult)
        gpsimd_step(gp_diff[:, first], vf_gp[:, first], product_sb[:, first], ALU.subtract)
        gpsimd_step(gp_result[:, second], gp_step[:, second], kept[:], ALU.add)
        gpsimd_store(second)
        gpsimd_step(gp_step[:, first], gp_diff[:, first], gate_sb[:, first], ALU.mult)
        gpsimd_step(gp_result[:, first], gp_step[:, first], product_sb[:, first], ALU.add)
        gpsimd_store(first)

        scale(1)
        subtract(2)
        finish(1)
        scale(2)
        subtract(3)
        finish(2)
        for cols in halves:
            nc.vector.tensor_tensor(
                out=step[3][:, cols], in0=diff[3][:, cols], in1=gate[3][:, cols], op=ALU.mult
            )
        for cols in halves:
            nc.vector.tensor_tensor(
                out=result[3][:, cols], in0=step[3][:, cols], in1=product[3][:, cols], op=ALU.add
            )
            nc.sync.dma_start(out=out_view[:, 3, cols], in_=result[3][:, cols])
